import numpy as np
import ml_dtypes


def mxq(x, axis, fmt="e4m3"):
    dtype, down = {"e4m3": (ml_dtypes.float8_e4m3fn, 7), "e5m2": (ml_dtypes.float8_e5m2, 14)}[fmt]
    v = np.moveaxis(np.asarray(x, np.float32).astype(ml_dtypes.bfloat16).astype(np.float64), axis, -1)
    blocks = v.reshape(v.shape[:-1] + (-1, 32))
    amax = np.abs(blocks).max(-1, keepdims=True)
    byte = np.maximum(np.where(amax > 0, np.frexp(amax)[1] - 1 + 127, 0) - down, 1)
    scale = np.exp2(byte - 127.0)
    codes = (blocks / scale).astype(np.float32).astype(dtype).astype(np.float64)
    return np.moveaxis((codes * scale).reshape(v.shape), -1, axis)


WIDE = False


def mx_kscale(k):
    if not WIDE:
        return np.ones(k)
    levels = np.array([10, -10, 5, -5, 0])
    a = np.random.permutation(np.resize(levels, k // 512 * 4)).reshape(k // 512, 4)
    idx = np.arange(k)
    return np.exp2(a[idx // 512, idx % 128 // 32])


BF16 = ml_dtypes.bfloat16


def bf(x):
    return np.asarray(x, np.float32).astype(BF16)


def f64(x):
    return np.asarray(x).astype(np.float64)


B, LI, LJ, LT, CIN, CD = 1, 512, 512, 512, 16, 8
EPS = 1e-5
SL = 2.4 / LT ** 0.25
MU = 3.4 / np.sqrt(LT)


def sigmoid(v):
    return 1.0 / (1.0 + np.exp(-v))


def setup_inputs():
    s = mx_kscale(LT)[None, None, :, None]
    mu_a = MU * (1.0 + 0.3 * np.random.standard_normal(CD))
    mu_b = MU * (1.0 + 0.3 * np.random.standard_normal(CD))
    return {
        "gate_a": bf(np.random.standard_normal((B, LI, LT, CD))),
        "lin_a": bf((SL * np.random.standard_normal((B, LI, LT, CD)) + mu_a) * s),
        "gate_b": bf(np.random.standard_normal((B, LJ, LT, CD))),
        "lin_b": bf((SL * np.random.standard_normal((B, LJ, LT, CD)) + mu_b) / s),
        "alpha_o": bf(1.3 + 0.1 * np.random.standard_normal(1)),
        "beta_o": bf(0.3 + 0.05 * np.random.standard_normal(1)),
    }


def reference(gate_a, lin_a, gate_b, lin_b, alpha_o, beta_o):
    a = sigmoid(f64(gate_a)) * f64(lin_a)
    b = sigmoid(f64(gate_b)) * f64(lin_b)
    at = np.ascontiguousarray(a.transpose(0, 3, 1, 2))
    bt = np.ascontiguousarray(b.transpose(0, 3, 2, 1))
    k = (mxq(at, 3, "e4m3") @ mxq(bt, 2, "e4m3")).transpose(0, 2, 3, 1)
    m = k.mean()
    v = k.var()
    nv = (k - m) * (1.0 / np.sqrt(v + EPS))
    return f64(alpha_o) * nv + f64(beta_o)

@@ -1,0 +1,201 @@
+from contextlib import ExitStack
+
+import concourse.bass as bass
+import concourse.mybir as mybir
+import concourse.tile as tile
+from concourse.masks import make_identity
+
+F32 = mybir.dt.float32
+BF16 = mybir.dt.bfloat16
+U32 = mybir.dt.uint32
+U8 = mybir.dt.uint8
+FP8X4 = mybir.dt.float8_e4m3fn_x4
+ACT = mybir.ActivationFunctionType
+ALU = mybir.AluOpType
+
+P = 128
+ROWS = 512
+LT = 512
+CD = 8
+EPS = 1e-5
+BLOCKS = ROWS // P
+PACK = 4
+PAIRS = CD // 2
+WORDS = LT * PAIRS
+BN_DIM = 6
+
+FLOPS = 2 * ROWS * ROWS * LT * CD
+
+
+def tile_sparstriangularupdate_pa_kernel(
+    tc, gate_a, lin_a, gate_b, lin_b, alpha_o, beta_o, out
+):
+    nc = tc.nc
+    with ExitStack() as ctx:
+        ctx.enter_context(tc.manual_schedule())
+        const = ctx.enter_context(tc.tile_pool(name="const", bufs=1))
+        keep = ctx.enter_context(tc.tile_pool(name="keep", bufs=1))
+
+        alpha_bf = const.tile([P, 1], BF16)
+        beta_bf = const.tile([P, 1], BF16)
+        with nc.allow_non_contiguous_dma(reason="one scalar to every partition"):
+            nc.scalar.dma_start(out=alpha_bf[:], in_=alpha_o.partition_broadcast(P))
+            nc.scalar.dma_start(out=beta_bf[:], in_=beta_o.partition_broadcast(P))
+        ident = const.tile([P, P], F32)
+        make_identity(nc, ident[:])
+        mean_weights = const.tile([P, P], F32)
+        nc.vector.memset(mean_weights[:], 1.0 / P)
+        minus_half = const.tile([P, 1], F32)
+        nc.vector.memset(minus_half[:], -0.5)
+
+        codes = {}
+        scales = {}
+        for side in ("a", "b"):
+            codes[side] = keep.tile([P, CD, ROWS], U32, name="codes_" + side, align_bytes=64)
+            scales[side] = keep.tile([P, CD, ROWS], U8, name="scales_" + side, align_bytes=64)
+        stats = keep.tile([P, BLOCKS * CD, BN_DIM], F32)
+
+        with ExitStack() as first:
+            raw = first.enter_context(tc.tile_pool(name="raw", bufs=1))
+            sig_pool = first.enter_context(tc.tile_pool(name="sig", bufs=3))
+            grp_pool = first.enter_context(tc.tile_pool(name="grp", bufs=3))
+            psum_t = first.enter_context(tc.psum_pool(name="psum_t", bufs=2))
+            psum_k = first.enter_context(tc.psum_pool(name="psum_k", bufs=3))
+
+            gate_sb = {}
+            lin_sb = {}
+            for side, gate, lin in (("b", gate_b, lin_b), ("a", gate_a, lin_a)):
+                for r in range(BLOCKS):
+                    rows = slice(r * P, (r + 1) * P)
+                    g = raw.tile([P, LT * CD], BF16, name="gate_%s%d" % (side, r))
+                    nc.sync.dma_start(out=g[:], in_=gate[0, rows].rearrange("p t c -> p (t c)"))
+                    l = raw.tile([P, LT * CD], BF16, name="lin_%s%d" % (side, r))
+                    nc.sync.dma_start(out=l[:], in_=lin[0, rows].rearrange("p t c -> p (t c)"))
+                    gate_sb[side, r] = g
+                    lin_sb[side, r] = l
+
+            units = [(side, r, q) for side in ("b", "a") for r in range(BLOCKS) for q in range(PAIRS)]
+            grouped_of = {}
+
+            def transpose_words(src, dst, q):
+                words = src[:].bitcast(F32).rearrange("p (u t q) -> p u q t", u=PACK, q=PAIRS)
+                for u in range(PACK):
+                    nc.tensor.transpose(dst[:, u * P : (u + 1) * P], words[:, u, q, :], ident[:])
+
+            def by_channel(bank):
+                return bank[:].bitcast(BF16).rearrange("p (u i e) -> p e i u", u=PACK, e=2)
+
+            def gate_and_multiply(unit):
+                side, r, q = unit
+                gate_t = psum_t.tile([P, PACK * P], F32, tag="gate_t")
+                transpose_words(gate_sb[side, r], gate_t, q)
+                lin_t = psum_t.tile([P, PACK * P], F32, tag="lin_t")
+                transpose_words(lin_sb[side, r], lin_t, q)
+                sig = sig_pool.tile([P, 2, P, PACK], F32, tag="sig")
+                nc.scalar.activation(out=sig[:], in_=by_channel(gate_t), func=ACT.Sigmoid)
+                grouped = grp_pool.tile([P, 2, P, PACK], BF16, tag="grouped", align_bytes=64)
+                nc.vector.tensor_tensor(out=grouped[:], in0=sig[:], in1=by_channel(lin_t), op=ALU.mult)
+                grouped_of[unit] = grouped
+
+            def quantise(unit):
+                side, r, q = unit
+                rows = slice(r * P, (r + 1) * P)
+                for e in range(2):
+                    nc.vector.quantize_mx(
+                        out=codes[side][:, 2 * q + e, rows].bitcast(FP8X4),
+                        scales=scales[side][:, 2 * q + e, rows],
+                        in_=grouped_of[unit][:, e].rearrange("p i u -> p (i u)"),
+                    )
+
+            def product_statistics(unit):
+                side, r, q = unit
+                rows = slice(r * P, (r + 1) * P)
+                for c in (2 * q, 2 * q + 1):
+                    k = psum_k.tile([P, ROWS], F32, tag="k")
+                    nc.tensor.matmul_mx(
+                        out=k[:],
+                        lhsT=codes["a"][:, c, rows].bitcast(FP8X4),
+                        lhsT_scale=scales["a"][:, c, rows],
+                        rhs=codes["b"][:, c, :].bitcast(FP8X4),
+                        rhs_scale=scales["b"][:, c, :],
+                        start=True,
+                        stop=True,
+                    )
+                    nc.vector.bn_stats(out=stats[:, r * CD + c, :], in_=k[:])
+
+            for n in range(len(units) + 2):
+                if n < len(units):
+                    gate_and_multiply(units[n])
+                if 1 <= n <= len(units):
+                    quantise(units[n - 1])
+                if n >= 2 and units[n - 2][0] == "a":
+                    product_statistics(units[n - 2])
+
+            moments = keep.tile([P, 2], F32)
+            nc.vector.bn_aggr(out=moments[:], in_=stats[:].rearrange("p n s -> p (n s)"))
+            nc.vector.scalar_tensor_tensor(
+                out=moments[:, 1:2], in0=moments[:, 0:1], scalar=moments[:, 0:1], in1=moments[:, 1:2],
+                op0=ALU.mult, op1=ALU.add,
+            )
+            total_ps = psum_t.tile([P, 2], F32, tag="gate_t")
+            nc.tensor.matmul(out=total_ps[:], lhsT=mean_weights[:], rhs=moments[:], start=True, stop=True)
+            total = keep.tile([P, 2], F32)
+            nc.vector.tensor_copy(out=total[:], in_=total_ps[:])
+
+        mean = total[:, 0:1]
+        neg_var = keep.tile([P, 1], F32)
+        nc.vector.scalar_tensor_tensor(
+            out=neg_var[:], in0=mean, scalar=mean, in1=total[:, 1:2], op0=ALU.mult, op1=ALU.subtract
+        )
+        var_eps = keep.tile([P, 1], F32)
+        nc.vector.tensor_scalar(
+            out=var_eps[:], in0=neg_var[:], scalar1=-1.0, scalar2=EPS, op0=ALU.mult, op1=ALU.add
+        )
+        rstd = keep.tile([P, 1], F32)
+        nc.gpsimd.tensor_tensor(out=rstd[:], in0=var_eps[:], in1=minus_half[:], op=ALU.pow)
+        neg_mean = keep.tile([P, 1], F32)
+        nc.vector.tensor_scalar(out=neg_mean[:], in0=mean, scalar1=-1.0, scalar2=None, op0=ALU.mult)
+        gain = keep.tile([P, 1], F32)
+        nc.vector.tensor_tensor(out=gain[:], in0=rstd[:], in1=alpha_bf[:], op=ALU.mult)
+        shift = keep.tile([P, 1], F32)
+        nc.vector.scalar_tensor_tensor(
+            out=shift[:], in0=neg_mean[:], scalar=gain[:, 0:1], in1=beta_bf[:], op0=ALU.mult, op1=ALU.add
+        )
+
+        HALF = CD // 2
+        with ExitStack() as second:
+            psum_o = second.enter_context(tc.psum_pool(name="psum_o", bufs=8, reuse_waits="tile"))
+            out_pool = second.enter_context(tc.tile_pool(name="out_sb", bufs=4, reuse_waits="tile"))
+            for r in range(BLOCKS):
+                rows = slice(r * P, (r + 1) * P)
+                for s in range(BLOCKS):
+                    cols = slice(s * P, (s + 1) * P)
+                    result = out_pool.tile([P, P, CD], F32, tag="result")
+                    for h in range(2):
+                        bank = psum_o.tile([P, HALF, P], F32, tag="bank")
+                        for x in range(HALF):
+                            c = h * HALF + x
+                            nc.tensor.matmul_mx(
+                                out=bank[:, x, :],
+                                lhsT=codes["a"][:, c, rows].bitcast(FP8X4),
+                                lhsT_scale=scales["a"][:, c, rows],
+                                rhs=codes["b"][:, c, cols].bitcast(FP8X4),
+                                rhs_scale=scales["b"][:, c, cols],
+                                start=True,
+                                stop=True,
+                            )
+                        src = bank[:].rearrange("p x j -> p j x")
+                        dst = result[:, :, h * HALF : (h + 1) * HALF]
+                        if (r * BLOCKS + s) % 2 == 0:
+                            nc.scalar.activation(
+                                out=dst, in_=src, func=ACT.Identity, bias=shift[:, 0:1], scale=gain[:, 0:1]
+                            )
+                        else:
+                            nc.vector.tensor_scalar(
+                                out=dst, in0=src, scalar1=gain[:, 0:1], scalar2=shift[:, 0:1],
+                                op0=ALU.mult, op1=ALU.add,
+                            )
+                    nc.sync.dma_start(
+                        out=out[0, rows, cols, :].rearrange("p j c -> p (j c)"),
+                        in_=result[:].rearrange("p j c -> p (j c)"),
+                    )

@@ -12,6 +12,7 @@ U8 = mybir.dt.uint8
 FP8X4 = mybir.dt.float8_e4m3fn_x4
 ACT = mybir.ActivationFunctionType
 ALU = mybir.AluOpType
+AX = mybir.AxisListType
 
 P = 128
 ROWS = 512
@@ -23,6 +24,7 @@ PACK = 4
 PAIRS = CD // 2
 WORDS = LT * PAIRS
 BN_DIM = 6
+ODD_COUNT = BLOCKS * PAIRS * ROWS
 
 FLOPS = 2 * ROWS * ROWS * LT * CD
 
@@ -44,7 +46,7 @@ def tile_sparstriangularupdate_pa_kernel(
         ident = const.tile([P, P], F32)
         make_identity(nc, ident[:])
         mean_weights = const.tile([P, P], F32)
-        nc.vector.memset(mean_weights[:], 1.0 / P)
+        nc.vector.memset(mean_weights[:], 1.0 / (ROWS * ROWS * CD))
         minus_half = const.tile([P, 1], F32)
         nc.vector.memset(minus_half[:], -0.5)
 
@@ -53,7 +55,9 @@ def tile_sparstriangularupdate_pa_kernel(
         for side in ("a", "b"):
             codes[side] = keep.tile([P, CD, ROWS], U32, name="codes_" + side, align_bytes=64)
             scales[side] = keep.tile([P, CD, ROWS], U8, name="scales_" + side, align_bytes=64)
-        stats = keep.tile([P, BLOCKS * CD, BN_DIM], F32)
+        stats = keep.tile([P, BLOCKS * PAIRS, BN_DIM], F32)
+        square_sums = keep.tile([P, BLOCKS * PAIRS], F32)
+        even_sum = keep.tile([P, 1], F32)
 
         with ExitStack() as first:
             raw = first.enter_context(tc.tile_pool(name="raw", bufs=1))
@@ -61,6 +65,9 @@ def tile_sparstriangularupdate_pa_kernel(
             grp_pool = first.enter_context(tc.tile_pool(name="grp", bufs=3))
             psum_t = first.enter_context(tc.psum_pool(name="psum_t", bufs=2))
             psum_k = first.enter_context(tc.psum_pool(name="psum_k", bufs=3))
+            psum_s = first.enter_context(tc.psum_pool(name="psum_s", bufs=1))
+            junk_pool = first.enter_context(tc.tile_pool(name="junk", bufs=3))
+            k_sum = psum_s.tile([P, ROWS], F32)
 
             gate_sb = {}
             lin_sb = {}
@@ -75,6 +82,8 @@ def tile_sparstriangularupdate_pa_kernel(
                     lin_sb[side, r] = l
 
             units = [(side, r, q) for side in ("b", "a") for r in range(BLOCKS) for q in range(PAIRS)]
+            lin_t_of = {}
+            sig_of = {}
             grouped_of = {}
 
             def transpose_words(src, dst, q):
@@ -85,7 +94,7 @@ def tile_sparstriangularupdate_pa_kernel(
             def by_channel(bank):
                 return bank[:].bitcast(BF16).rearrange("p (u i e) -> p e i u", u=PACK, e=2)
 
-            def gate_and_multiply(unit):
+            def transpose_and_gate(unit):
                 side, r, q = unit
                 gate_t = psum_t.tile([P, PACK * P], F32, tag="gate_t")
                 transpose_words(gate_sb[side, r], gate_t, q)
@@ -93,8 +102,14 @@ def tile_sparstriangularupdate_pa_kernel(
                 transpose_words(lin_sb[side, r], lin_t, q)
                 sig = sig_pool.tile([P, 2, P, PACK], F32, tag="sig")
                 nc.scalar.activation(out=sig[:], in_=by_channel(gate_t), func=ACT.Sigmoid)
+                lin_t_of[unit] = lin_t
+                sig_of[unit] = sig
+
+            def multiply(unit):
                 grouped = grp_pool.tile([P, 2, P, PACK], BF16, tag="grouped", align_bytes=64)
-                nc.vector.tensor_tensor(out=grouped[:], in0=sig[:], in1=by_channel(lin_t), op=ALU.mult)
+                nc.vector.tensor_tensor(
+                    out=grouped[:], in0=sig_of[unit][:], in1=by_channel(lin_t_of[unit]), op=ALU.mult
+                )
                 grouped_of[unit] = grouped
 
             def quantise(unit):
@@ -107,34 +122,61 @@ def tile_sparstriangularupdate_pa_kernel(
                         in_=grouped_of[unit][:, e].rearrange("p i u -> p (i u)"),
                     )
 
+            def product(dst, r, c, start, stop):
+                rows = slice(r * P, (r + 1) * P)
+                nc.tensor.matmul_mx(
+                    out=dst,
+                    lhsT=codes["a"][:, c, rows].bitcast(FP8X4),
+                    lhsT_scale=scales["a"][:, c, rows],
+                    rhs=codes["b"][:, c, :].bitcast(FP8X4),
+                    rhs_scale=scales["b"][:, c, :],
+                    start=start,
+                    stop=stop,
+                )
+
             def product_statistics(unit):
                 side, r, q = unit
-                rows = slice(r * P, (r + 1) * P)
-                for c in (2 * q, 2 * q + 1):
-                    k = psum_k.tile([P, ROWS], F32, tag="k")
-                    nc.tensor.matmul_mx(
-                        out=k[:],
-                        lhsT=codes["a"][:, c, rows].bitcast(FP8X4),
-                        lhsT_scale=scales["a"][:, c, rows],
-                        rhs=codes["b"][:, c, :].bitcast(FP8X4),
-                        rhs_scale=scales["b"][:, c, :],
-                        start=True,
-                        stop=True,
-                    )
-                    nc.vector.bn_stats(out=stats[:, r * CD + c, :], in_=k[:])
+                n = r * PAIRS + q
+                k_even = psum_k.tile([P, ROWS], F32, tag="k")
+                product(k_even[:], r, 2 * q, True, True)
+                product(k_sum[:], r, 2 * q, n == 0, n == BLOCKS * PAIRS - 1)
+                k_odd = psum_k.tile([P, ROWS], F32, tag="k")
+                product(k_odd[:], r, 2 * q + 1, True, True)
+                junk = junk_pool.tile([P, ROWS], BF16, tag="junk")
+                nc.scalar.activation(
+                    out=junk[:], in_=k_even[:], func=ACT.Square, accum_out=square_sums[:, n : n + 1]
+                )
+                nc.vector.bn_stats(out=stats[:, n, :], in_=k_odd[:])
 
-            for n in range(len(units) + 2):
-                if n < len(units):
-                    gate_and_multiply(units[n])
-                if 1 <= n <= len(units):
+            count = len(units)
+            for n in range(-1, count + 2):
+                if n + 1 < count:
+                    transpose_and_gate(units[n + 1])
+                if 0 <= n < count:
+                    multiply(units[n])
+                if 0 <= n - 1 < count:
                     quantise(units[n - 1])
-                if n >= 2 and units[n - 2][0] == "a":
+                if 0 <= n - 2 and units[n - 2][0] == "a":
                     product_statistics(units[n - 2])
 
-            moments = keep.tile([P, 2], F32)
-            nc.vector.bn_aggr(out=moments[:], in_=stats[:].rearrange("p n s -> p (n s)"))
+            junk = junk_pool.tile([P, ROWS], BF16, tag="junk")
+            nc.scalar.activation(out=junk[:], in_=k_sum[:], func=ACT.Identity, accum_out=even_sum[:])
+            odd = keep.tile([P, 2], F32)
+            nc.vector.bn_aggr(out=odd[:], in_=stats[:].rearrange("p n s -> p (n s)"))
+            even_squares = keep.tile([P, 1], F32)
+            nc.vector.tensor_reduce(out=even_squares[:], in_=square_sums[:], axis=AX.X, op=ALU.add)
+            odd_square = keep.tile([P, 1], F32)
             nc.vector.scalar_tensor_tensor(
-                out=moments[:, 1:2], in0=moments[:, 0:1], scalar=moments[:, 0:1], in1=moments[:, 1:2],
+                out=odd_square[:], in0=odd[:, 0:1], scalar=odd[:, 0:1], in1=odd[:, 1:2],
+                op0=ALU.mult, op1=ALU.add,
+            )
+            moments = keep.tile([P, 2], F32)
+            nc.vector.scalar_tensor_tensor(
+                out=moments[:, 1:2], in0=odd_square[:], scalar=float(ODD_COUNT), in1=even_squares[:],
+                op0=ALU.mult, op1=ALU.add,
+            )
+            nc.vector.scalar_tensor_tensor(
+                out=moments[:, 0:1], in0=odd[:, 0:1], scalar=float(ODD_COUNT), in1=even_sum[:],
                 op0=ALU.mult, op1=ALU.add,
             )
             total_ps = psum_t.tile([P, 2], F32, tag="gate_t")

@@ -1,8 +1,6 @@
 from contextlib import ExitStack
 
-import concourse.bass as bass
 import concourse.mybir as mybir
-import concourse.tile as tile
 from concourse.masks import make_identity
 
 F32 = mybir.dt.float32
@@ -22,9 +20,14 @@ EPS = 1e-5
 BLOCKS = ROWS // P
 PACK = 4
 PAIRS = CD // 2
-WORDS = LT * PAIRS
+HALF = CD // 2
 BN_DIM = 6
-ODD_COUNT = BLOCKS * PAIRS * ROWS
+A_UNITS = BLOCKS * PAIRS
+ODD_COUNT = A_UNITS * ROWS
+COUNT = ROWS * ROWS * CD
+STEP = 2
+BLOCK_F32 = 8
+AHEAD = 2
 
 FLOPS = 2 * ROWS * ROWS * LT * CD
 
@@ -38,35 +41,47 @@ def tile_sparstriangularupdate_pa_kernel(
         const = ctx.enter_context(tc.tile_pool(name="const", bufs=1))
         keep = ctx.enter_context(tc.tile_pool(name="keep", bufs=1))
 
-        alpha_bf = const.tile([P, 1], BF16)
-        beta_bf = const.tile([P, 1], BF16)
-        with nc.allow_non_contiguous_dma(reason="one scalar to every partition"):
-            nc.scalar.dma_start(out=alpha_bf[:], in_=alpha_o.partition_broadcast(P))
-            nc.scalar.dma_start(out=beta_bf[:], in_=beta_o.partition_broadcast(P))
         ident = const.tile([P, P], F32)
         make_identity(nc, ident[:])
-        mean_weights = const.tile([P, P], F32)
-        nc.vector.memset(mean_weights[:], 1.0 / (ROWS * ROWS * CD))
+        even_weights = const.tile([P, P], F32)
+        nc.vector.memset(even_weights[:], 1.0 / COUNT)
+        odd_weights = const.tile([P, P], F32)
+        nc.vector.memset(odd_weights[:], float(ODD_COUNT) / COUNT)
         minus_half = const.tile([P, 1], F32)
         nc.vector.memset(minus_half[:], -0.5)
+        alpha_bf = const.tile([P, 1], BF16)
+        beta_bf = const.tile([P, 1], BF16)
 
         codes = {}
         scales = {}
         for side in ("a", "b"):
             codes[side] = keep.tile([P, CD, ROWS], U32, name="codes_" + side, align_bytes=64)
             scales[side] = keep.tile([P, CD, ROWS], U8, name="scales_" + side, align_bytes=64)
-        stats = keep.tile([P, BLOCKS * PAIRS, BN_DIM], F32)
-        square_sums = keep.tile([P, BLOCKS * PAIRS], F32)
-        even_sum = keep.tile([P, 1], F32)
+
+        def product(dst, c, rows, cols, start, stop):
+            nc.tensor.matmul_mx(
+                out=dst,
+                lhsT=codes["a"][:, c, rows].bitcast(FP8X4),
+                lhsT_scale=scales["a"][:, c, rows],
+                rhs=codes["b"][:, c, cols].bitcast(FP8X4),
+                rhs_scale=scales["b"][:, c, cols],
+                start=start,
+                stop=stop,
+            )
+
+        odd_stats = keep.tile([P, A_UNITS, BN_DIM], F32)
+        square_sums = keep.tile([P, A_UNITS], F32)
+        odd = keep.tile([P, 2], F32)
+        even = keep.tile([P, 2, BLOCK_F32], F32)
 
         with ExitStack() as first:
             raw = first.enter_context(tc.tile_pool(name="raw", bufs=1))
-            sig_pool = first.enter_context(tc.tile_pool(name="sig", bufs=3))
-            grp_pool = first.enter_context(tc.tile_pool(name="grp", bufs=3))
-            psum_t = first.enter_context(tc.psum_pool(name="psum_t", bufs=2))
+            sig_pool = first.enter_context(tc.tile_pool(name="sig", bufs=2 * STEP))
+            grp_pool = first.enter_context(tc.tile_pool(name="grp", bufs=2 * STEP))
+            junk_pool = first.enter_context(tc.tile_pool(name="junk", bufs=3))
+            psum_t = first.enter_context(tc.psum_pool(name="psum_t", bufs=STEP))
             psum_k = first.enter_context(tc.psum_pool(name="psum_k", bufs=3))
             psum_s = first.enter_context(tc.psum_pool(name="psum_s", bufs=1))
-            junk_pool = first.enter_context(tc.tile_pool(name="junk", bufs=3))
             k_sum = psum_s.tile([P, ROWS], F32)
 
             gate_sb = {}
@@ -80,8 +95,11 @@ def tile_sparstriangularupdate_pa_kernel(
                     nc.sync.dma_start(out=l[:], in_=lin[0, rows].rearrange("p t c -> p (t c)"))
                     gate_sb[side, r] = g
                     lin_sb[side, r] = l
+            with nc.allow_non_contiguous_dma(reason="one scalar to every partition"):
+                nc.sync.dma_start(out=alpha_bf[:], in_=alpha_o.partition_broadcast(P))
+                nc.sync.dma_start(out=beta_bf[:], in_=beta_o.partition_broadcast(P))
 
-            units = [(side, r, q) for side in ("b", "a") for r in range(BLOCKS) for q in range(PAIRS)]
+            gate_t_of = {}
             lin_t_of = {}
             sig_of = {}
             grouped_of = {}
@@ -94,15 +112,21 @@ def tile_sparstriangularupdate_pa_kernel(
             def by_channel(bank):
                 return bank[:].bitcast(BF16).rearrange("p (u i e) -> p e i u", u=PACK, e=2)
 
-            def transpose_and_gate(unit):
+            def transpose_gate(unit):
                 side, r, q = unit
                 gate_t = psum_t.tile([P, PACK * P], F32, tag="gate_t")
                 transpose_words(gate_sb[side, r], gate_t, q)
+                gate_t_of[unit] = gate_t
+
+            def transpose_lin(unit):
+                side, r, q = unit
                 lin_t = psum_t.tile([P, PACK * P], F32, tag="lin_t")
                 transpose_words(lin_sb[side, r], lin_t, q)
-                sig = sig_pool.tile([P, 2, P, PACK], F32, tag="sig")
-                nc.scalar.activation(out=sig[:], in_=by_channel(gate_t), func=ACT.Sigmoid)
                 lin_t_of[unit] = lin_t
+
+            def sigmoid(unit):
+                sig = sig_pool.tile([P, 2, P, PACK], F32, tag="sig")
+                nc.scalar.activation(out=sig[:], in_=by_channel(gate_t_of[unit]), func=ACT.Sigmoid)
                 sig_of[unit] = sig
 
             def multiply(unit):
@@ -122,68 +146,77 @@ def tile_sparstriangularupdate_pa_kernel(
                         in_=grouped_of[unit][:, e].rearrange("p i u -> p (i u)"),
                     )
 
-            def product(dst, r, c, start, stop):
-                rows = slice(r * P, (r + 1) * P)
-                nc.tensor.matmul_mx(
-                    out=dst,
-                    lhsT=codes["a"][:, c, rows].bitcast(FP8X4),
-                    lhsT_scale=scales["a"][:, c, rows],
-                    rhs=codes["b"][:, c, :].bitcast(FP8X4),
-                    rhs_scale=scales["b"][:, c, :],
-                    start=start,
-                    stop=stop,
-                )
-
             def product_statistics(unit):
                 side, r, q = unit
                 n = r * PAIRS + q
+                rows = slice(r * P, (r + 1) * P)
+                every_j = slice(0, ROWS)
                 k_even = psum_k.tile([P, ROWS], F32, tag="k")
-                product(k_even[:], r, 2 * q, True, True)
-                product(k_sum[:], r, 2 * q, n == 0, n == BLOCKS * PAIRS - 1)
+                product(k_even[:], 2 * q, rows, every_j, True, True)
+                product(k_sum[:], 2 * q, rows, every_j, n == 0, n == A_UNITS - 1)
                 k_odd = psum_k.tile([P, ROWS], F32, tag="k")
-                product(k_odd[:], r, 2 * q + 1, True, True)
+                product(k_odd[:], 2 * q + 1, rows, every_j, True, True)
                 junk = junk_pool.tile([P, ROWS], BF16, tag="junk")
                 nc.scalar.activation(
                     out=junk[:], in_=k_even[:], func=ACT.Square, accum_out=square_sums[:, n : n + 1]
                 )
-                nc.vector.bn_stats(out=stats[:, n, :], in_=k_odd[:])
+                nc.vector.bn_stats(out=odd_stats[:, n, :], in_=k_odd[:])
 
-            count = len(units)
-            for n in range(-1, count + 2):
-                if n + 1 < count:
-                    transpose_and_gate(units[n + 1])
-                if 0 <= n < count:
-                    multiply(units[n])
-                if 0 <= n - 1 < count:
-                    quantise(units[n - 1])
-                if 0 <= n - 2 and units[n - 2][0] == "a":
-                    product_statistics(units[n - 2])
+            units = [(side, r, q) for side in ("b", "a") for r in range(BLOCKS) for q in range(PAIRS)]
+            steps = [units[n : n + STEP] for n in range(0, len(units), STEP)]
+            for p in range(len(steps) + 1):
+                if p < len(steps):
+                    for unit in steps[p]:
+                        transpose_gate(unit)
+                    for unit in steps[p]:
+                        transpose_lin(unit)
+                    for unit in steps[p]:
+                        sigmoid(unit)
+                    for unit in steps[p]:
+                        multiply(unit)
+                    for unit in steps[p]:
+                        quantise(unit)
+                if p >= 1 and steps[p - 1][0][0] == "a":
+                    for unit in steps[p - 1]:
+                        product_statistics(unit)
 
             junk = junk_pool.tile([P, ROWS], BF16, tag="junk")
-            nc.scalar.activation(out=junk[:], in_=k_sum[:], func=ACT.Identity, accum_out=even_sum[:])
-            odd = keep.tile([P, 2], F32)
-            nc.vector.bn_aggr(out=odd[:], in_=stats[:].rearrange("p n s -> p (n s)"))
-            even_squares = keep.tile([P, 1], F32)
-            nc.vector.tensor_reduce(out=even_squares[:], in_=square_sums[:], axis=AX.X, op=ALU.add)
-            odd_square = keep.tile([P, 1], F32)
+            nc.scalar.activation(
+                out=junk[:], in_=k_sum[:], func=ACT.Identity, accum_out=even[:, 0, 0:1]
+            )
+            nc.vector.bn_aggr(out=odd[:], in_=odd_stats[:].rearrange("p n s -> p (n s)"))
             nc.vector.scalar_tensor_tensor(
-                out=odd_square[:], in0=odd[:, 0:1], scalar=odd[:, 0:1], in1=odd[:, 1:2],
+                out=odd[:, 1:2], in0=odd[:, 0:1], scalar=odd[:, 0:1], in1=odd[:, 1:2],
                 op0=ALU.mult, op1=ALU.add,
             )
-            moments = keep.tile([P, 2], F32)
-            nc.vector.scalar_tensor_tensor(
-                out=moments[:, 1:2], in0=odd_square[:], scalar=float(ODD_COUNT), in1=even_squares[:],
-                op0=ALU.mult, op1=ALU.add,
-            )
-            nc.vector.scalar_tensor_tensor(
-                out=moments[:, 0:1], in0=odd[:, 0:1], scalar=float(ODD_COUNT), in1=even_sum[:],
-                op0=ALU.mult, op1=ALU.add,
-            )
-            total_ps = psum_t.tile([P, 2], F32, tag="gate_t")
-            nc.tensor.matmul(out=total_ps[:], lhsT=mean_weights[:], rhs=moments[:], start=True, stop=True)
-            total = keep.tile([P, 2], F32)
-            nc.vector.tensor_copy(out=total[:], in_=total_ps[:])
+            nc.vector.tensor_reduce(out=even[:, 1, 0:1], in_=square_sums[:], axis=AX.X, op=ALU.add)
 
+        psum_o = ctx.enter_context(tc.psum_pool(name="psum_o", bufs=8, reuse_waits="tile"))
+        out_pool = ctx.enter_context(tc.tile_pool(name="out_sb", bufs=4, reuse_waits="tile"))
+        banks_of = {}
+
+        def form_products(n):
+            r, s = divmod(n, BLOCKS)
+            banks_of[n] = []
+            for h in range(2):
+                bank = psum_o.tile([P, HALF, P], F32, tag="bank")
+                for x in range(HALF):
+                    product(
+                        bank[:, x, :], h * HALF + x, slice(r * P, (r + 1) * P),
+                        slice(s * P, (s + 1) * P), True, True,
+                    )
+                banks_of[n].append(bank)
+
+        for n in range(AHEAD):
+            form_products(n)
+
+        total_ps = psum_o.tile([P, 2], F32, tag="bank")
+        nc.tensor.matmul(out=total_ps[:], lhsT=odd_weights[:], rhs=odd[:], start=True, stop=False)
+        nc.tensor.matmul(
+            out=total_ps[:], lhsT=even_weights[:], rhs=even[:, :, 0], start=False, stop=True
+        )
+        total = keep.tile([P, 2], F32)
+        nc.vector.tensor_copy(out=total[:], in_=total_ps[:])
         mean = total[:, 0:1]
         neg_var = keep.tile([P, 1], F32)
         nc.vector.scalar_tensor_tensor(
@@ -204,40 +237,24 @@ def tile_sparstriangularupdate_pa_kernel(
             out=shift[:], in0=neg_mean[:], scalar=gain[:, 0:1], in1=beta_bf[:], op0=ALU.mult, op1=ALU.add
         )
 
-        HALF = CD // 2
-        with ExitStack() as second:
-            psum_o = second.enter_context(tc.psum_pool(name="psum_o", bufs=8, reuse_waits="tile"))
-            out_pool = second.enter_context(tc.tile_pool(name="out_sb", bufs=4, reuse_waits="tile"))
-            for r in range(BLOCKS):
-                rows = slice(r * P, (r + 1) * P)
-                for s in range(BLOCKS):
-                    cols = slice(s * P, (s + 1) * P)
-                    result = out_pool.tile([P, P, CD], F32, tag="result")
-                    for h in range(2):
-                        bank = psum_o.tile([P, HALF, P], F32, tag="bank")
-                        for x in range(HALF):
-                            c = h * HALF + x
-                            nc.tensor.matmul_mx(
-                                out=bank[:, x, :],
-                                lhsT=codes["a"][:, c, rows].bitcast(FP8X4),
-                                lhsT_scale=scales["a"][:, c, rows],
-                                rhs=codes["b"][:, c, cols].bitcast(FP8X4),
-                                rhs_scale=scales["b"][:, c, cols],
-                                start=True,
-                                stop=True,
-                            )
-                        src = bank[:].rearrange("p x j -> p j x")
-                        dst = result[:, :, h * HALF : (h + 1) * HALF]
-                        if (r * BLOCKS + s) % 2 == 0:
-                            nc.scalar.activation(
-                                out=dst, in_=src, func=ACT.Identity, bias=shift[:, 0:1], scale=gain[:, 0:1]
-                            )
-                        else:
-                            nc.vector.tensor_scalar(
-                                out=dst, in0=src, scalar1=gain[:, 0:1], scalar2=shift[:, 0:1],
-                                op0=ALU.mult, op1=ALU.add,
-                            )
-                    nc.sync.dma_start(
-                        out=out[0, rows, cols, :].rearrange("p j c -> p (j c)"),
-                        in_=result[:].rearrange("p j c -> p (j c)"),
+        for n in range(BLOCKS * BLOCKS):
+            r, s = divmod(n, BLOCKS)
+            result = out_pool.tile([P, P, CD], F32, tag="result")
+            for h in range(2):
+                src = banks_of[n][h][:].rearrange("p x j -> p j x")
+                dst = result[:, :, h * HALF : (h + 1) * HALF]
+                if n % 2 == 0:
+                    nc.scalar.activation(
+                        out=dst, in_=src, func=ACT.Identity, bias=shift[:, 0:1], scale=gain[:, 0:1]
                     )
+                else:
+                    nc.vector.tensor_scalar(
+                        out=dst, in0=src, scalar1=gain[:, 0:1], scalar2=shift[:, 0:1],
+                        op0=ALU.mult, op1=ALU.add,
+                    )
+            nc.sync.dma_start(
+                out=out[0, r * P : (r + 1) * P, s * P : (s + 1) * P, :].rearrange("p j c -> p (j c)"),
+                in_=result[:].rearrange("p j c -> p (j c)"),
+            )
+            if n + AHEAD < BLOCKS * BLOCKS:
+                form_products(n + AHEAD)

@@ -25,7 +25,6 @@ BN_DIM = 6
 A_UNITS = BLOCKS * PAIRS
 ODD_COUNT = A_UNITS * ROWS
 COUNT = ROWS * ROWS * CD
-STEP = 2
 BLOCK_F32 = 8
 AHEAD = 2
 
@@ -76,10 +75,10 @@ def tile_sparstriangularupdate_pa_kernel(
 
         with ExitStack() as first:
             raw = first.enter_context(tc.tile_pool(name="raw", bufs=1))
-            sig_pool = first.enter_context(tc.tile_pool(name="sig", bufs=2 * STEP))
-            grp_pool = first.enter_context(tc.tile_pool(name="grp", bufs=2 * STEP))
+            sig_pool = first.enter_context(tc.tile_pool(name="sig", bufs=4))
+            grp_pool = first.enter_context(tc.tile_pool(name="grp", bufs=3))
             junk_pool = first.enter_context(tc.tile_pool(name="junk", bufs=3))
-            psum_t = first.enter_context(tc.psum_pool(name="psum_t", bufs=STEP))
+            psum_t = first.enter_context(tc.psum_pool(name="psum_t", bufs=2))
             psum_k = first.enter_context(tc.psum_pool(name="psum_k", bufs=3))
             psum_s = first.enter_context(tc.psum_pool(name="psum_s", bufs=1))
             k_sum = psum_s.tile([P, ROWS], F32)
@@ -163,22 +162,19 @@ def tile_sparstriangularupdate_pa_kernel(
                 nc.vector.bn_stats(out=odd_stats[:, n, :], in_=k_odd[:])
 
             units = [(side, r, q) for side in ("b", "a") for r in range(BLOCKS) for q in range(PAIRS)]
-            steps = [units[n : n + STEP] for n in range(0, len(units), STEP)]
-            for p in range(len(steps) + 1):
-                if p < len(steps):
-                    for unit in steps[p]:
-                        transpose_gate(unit)
-                    for unit in steps[p]:
-                        transpose_lin(unit)
-                    for unit in steps[p]:
-                        sigmoid(unit)
-                    for unit in steps[p]:
-                        multiply(unit)
-                    for unit in steps[p]:
-                        quantise(unit)
-                if p >= 1 and steps[p - 1][0][0] == "a":
-                    for unit in steps[p - 1]:
-                        product_statistics(unit)
+            count = len(units)
+            for n in range(-2, count + 2):
+                if n + 2 < count:
+                    transpose_gate(units[n + 2])
+                    sigmoid(units[n + 2])
+                if 0 <= n + 1 < count:
+                    transpose_lin(units[n + 1])
+                if 0 <= n < count:
+                    multiply(units[n])
+                if 0 <= n - 1 < count:
+                    quantise(units[n - 1])
+                if 0 <= n - 2 and units[n - 2][0] == "a":
+                    product_statistics(units[n - 2])
 
             junk = junk_pool.tile([P, ROWS], BF16, tag="junk")
             nc.scalar.activation(
@@ -244,13 +240,13 @@ def tile_sparstriangularupdate_pa_kernel(
                 src = banks_of[n][h][:].rearrange("p x j -> p j x")
                 dst = result[:, :, h * HALF : (h + 1) * HALF]
                 if n % 2 == 0:
-                    nc.scalar.activation(
-                        out=dst, in_=src, func=ACT.Identity, bias=shift[:, 0:1], scale=gain[:, 0:1]
-                    )
-                else:
                     nc.vector.tensor_scalar(
                         out=dst, in0=src, scalar1=gain[:, 0:1], scalar2=shift[:, 0:1],
                         op0=ALU.mult, op1=ALU.add,
+                    )
+                else:
+                    nc.scalar.activation(
+                        out=dst, in_=src, func=ACT.Identity, bias=shift[:, 0:1], scale=gain[:, 0:1]
                     )
             nc.sync.dma_start(
                 out=out[0, r * P : (r + 1) * P, s * P : (s + 1) * P, :].rearrange("p j c -> p (j c)"),

@@ -22,8 +22,7 @@ PACK = 4
 PAIRS = CD // 2
 HALF = CD // 2
 BN_DIM = 6
-A_UNITS = BLOCKS * PAIRS
-ODD_COUNT = A_UNITS * ROWS
+BANK_JOBS = 4
 COUNT = ROWS * ROWS * CD
 BLOCK_F32 = 8
 AHEAD = 2
@@ -42,10 +41,30 @@ def tile_sparstriangularupdate_pa_kernel(
 
         ident = const.tile([P, P], F32)
         make_identity(nc, ident[:])
+        block_order = [(side, r) for r in range(BLOCKS) for side in ("b", "a")]
+        units = [(side, r, q) for side, r in block_order for q in range(PAIRS)]
+        count = len(units)
+        banks_after = []
+        waiting = []
+        for n, (side, r, q) in enumerate(units):
+            partners = [x for other, x in block_order[: n // PAIRS] if other != side]
+            for x in partners:
+                for e in range(2):
+                    waiting.append((r, x, 2 * q + e) if side == "a" else (x, r, 2 * q + e))
+            full = []
+            while len(waiting) >= BANK_JOBS:
+                full.append((waiting[:BANK_JOBS], "scalar" if len(full) == 0 else "vector"))
+                waiting = waiting[BANK_JOBS:]
+            banks_after.append(full)
+        assert len(waiting) == 0
+        scalar_banks = sum(1 for full in banks_after for bank in full if bank[1] == "scalar")
+        vector_banks = sum(1 for full in banks_after for bank in full if bank[1] == "vector")
+        vector_count = vector_banks * BANK_JOBS * P
+
         even_weights = const.tile([P, P], F32)
         nc.vector.memset(even_weights[:], 1.0 / COUNT)
         odd_weights = const.tile([P, P], F32)
-        nc.vector.memset(odd_weights[:], float(ODD_COUNT) / COUNT)
+        nc.vector.memset(odd_weights[:], float(vector_count) / COUNT)
         minus_half = const.tile([P, 1], F32)
         nc.vector.memset(minus_half[:], -0.5)
         alpha_bf = const.tile([P, 1], BF16)
@@ -68,8 +87,8 @@ def tile_sparstriangularupdate_pa_kernel(
                 stop=stop,
             )
 
-        odd_stats = keep.tile([P, A_UNITS, BN_DIM], F32)
-        square_sums = keep.tile([P, A_UNITS], F32)
+        odd_stats = keep.tile([P, vector_banks, BN_DIM], F32)
+        square_sums = keep.tile([P, scalar_banks], F32)
         odd = keep.tile([P, 2], F32)
         even = keep.tile([P, 2, BLOCK_F32], F32)
 
@@ -81,19 +100,19 @@ def tile_sparstriangularupdate_pa_kernel(
             psum_t = first.enter_context(tc.psum_pool(name="psum_t", bufs=2))
             psum_k = first.enter_context(tc.psum_pool(name="psum_k", bufs=3))
             psum_s = first.enter_context(tc.psum_pool(name="psum_s", bufs=1))
-            k_sum = psum_s.tile([P, ROWS], F32)
+            k_sum = psum_s.tile([P, P], F32)
 
             gate_sb = {}
             lin_sb = {}
-            for side, gate, lin in (("b", gate_b, lin_b), ("a", gate_a, lin_a)):
-                for r in range(BLOCKS):
-                    rows = slice(r * P, (r + 1) * P)
-                    g = raw.tile([P, LT * CD], BF16, name="gate_%s%d" % (side, r))
-                    nc.sync.dma_start(out=g[:], in_=gate[0, rows].rearrange("p t c -> p (t c)"))
-                    l = raw.tile([P, LT * CD], BF16, name="lin_%s%d" % (side, r))
-                    nc.sync.dma_start(out=l[:], in_=lin[0, rows].rearrange("p t c -> p (t c)"))
-                    gate_sb[side, r] = g
-                    lin_sb[side, r] = l
+            for side, r in block_order:
+                gate, lin = (gate_b, lin_b) if side == "b" else (gate_a, lin_a)
+                rows = slice(r * P, (r + 1) * P)
+                g = raw.tile([P, LT * CD], BF16, name="gate_%s%d" % (side, r))
+                nc.sync.dma_start(out=g[:], in_=gate[0, rows].rearrange("p t c -> p (t c)"))
+                l = raw.tile([P, LT * CD], BF16, name="lin_%s%d" % (side, r))
+                nc.sync.dma_start(out=l[:], in_=lin[0, rows].rearrange("p t c -> p (t c)"))
+                gate_sb[side, r] = g
+                lin_sb[side, r] = l
             with nc.allow_non_contiguous_dma(reason="one scalar to every partition"):
                 nc.sync.dma_start(out=alpha_bf[:], in_=alpha_o.partition_broadcast(P))
                 nc.sync.dma_start(out=beta_bf[:], in_=beta_o.partition_broadcast(P))
@@ -145,24 +164,30 @@ def tile_sparstriangularupdate_pa_kernel(
                         in_=grouped_of[unit][:, e].rearrange("p i u -> p (i u)"),
                     )
 
-            def product_statistics(unit):
-                side, r, q = unit
-                n = r * PAIRS + q
-                rows = slice(r * P, (r + 1) * P)
-                every_j = slice(0, ROWS)
-                k_even = psum_k.tile([P, ROWS], F32, tag="k")
-                product(k_even[:], 2 * q, rows, every_j, True, True)
-                product(k_sum[:], 2 * q, rows, every_j, n == 0, n == A_UNITS - 1)
-                k_odd = psum_k.tile([P, ROWS], F32, tag="k")
-                product(k_odd[:], 2 * q + 1, rows, every_j, True, True)
-                junk = junk_pool.tile([P, ROWS], BF16, tag="junk")
-                nc.scalar.activation(
-                    out=junk[:], in_=k_even[:], func=ACT.Square, accum_out=square_sums[:, n : n + 1]
-                )
-                nc.vector.bn_stats(out=odd_stats[:, n, :], in_=k_odd[:])
+            done = {"scalar": 0, "vector": 0}
 
-            units = [(side, r, q) for side in ("b", "a") for r in range(BLOCKS) for q in range(PAIRS)]
-            count = len(units)
+            def product_statistics(jobs, engine):
+                i = done[engine]
+                done[engine] = i + 1
+                k = psum_k.tile([P, BANK_JOBS, P], F32, tag="k")
+                for x, (r, s, c) in enumerate(jobs):
+                    rows = slice(r * P, (r + 1) * P)
+                    cols = slice(s * P, (s + 1) * P)
+                    product(k[:, x, :], c, rows, cols, True, True)
+                    if engine == "scalar":
+                        product(
+                            k_sum[:], c, rows, cols, i == 0 and x == 0,
+                            i == scalar_banks - 1 and x == BANK_JOBS - 1,
+                        )
+                values = k[:].rearrange("p x j -> p (x j)")
+                if engine == "scalar":
+                    junk = junk_pool.tile([P, ROWS], BF16, tag="junk")
+                    nc.scalar.activation(
+                        out=junk[:], in_=values, func=ACT.Square, accum_out=square_sums[:, i : i + 1]
+                    )
+                else:
+                    nc.vector.bn_stats(out=odd_stats[:, i, :], in_=values)
+
             for n in range(-2, count + 2):
                 if n + 2 < count:
                     transpose_gate(units[n + 2])
@@ -173,12 +198,13 @@ def tile_sparstriangularupdate_pa_kernel(
                     multiply(units[n])
                 if 0 <= n - 1 < count:
                     quantise(units[n - 1])
-                if 0 <= n - 2 and units[n - 2][0] == "a":
-                    product_statistics(units[n - 2])
+                if 0 <= n - 2:
+                    for jobs, engine in banks_after[n - 2]:
+                        product_statistics(jobs, engine)
 
             junk = junk_pool.tile([P, ROWS], BF16, tag="junk")
             nc.scalar.activation(
-                out=junk[:], in_=k_sum[:], func=ACT.Identity, accum_out=even[:, 0, 0:1]
+                out=junk[:, 0:P], in_=k_sum[:], func=ACT.Identity, accum_out=even[:, 0, 0:1]
             )
             nc.vector.bn_aggr(out=odd[:], in_=odd_stats[:].rearrange("p n s -> p (n s)"))
             nc.vector.scalar_tensor_tensor(

@@ -25,6 +25,8 @@ BN_DIM = 6
 BANK_JOBS = 4
 COUNT = ROWS * ROWS * CD
 BLOCK_F32 = 8
+WARM_START = 6
+WARM_ROUND = 2
 AHEAD = 2
 
 FLOPS = 2 * ROWS * ROWS * LT * CD
@@ -164,6 +166,13 @@ def tile_sparstriangularupdate_pa_kernel(
                         in_=grouped_of[unit][:, e].rearrange("p i u -> p (i u)"),
                     )
 
+            def keep_warm(times):
+                unread = psum_k.tile([P, BANK_JOBS, P], F32, tag="k")
+                for x in range(times):
+                    nc.tensor.matmul(
+                        out=unread[:, x % BANK_JOBS, :], lhsT=ident[:], rhs=ident[:], start=True, stop=True
+                    )
+
             done = {"scalar": 0, "vector": 0}
 
             def product_statistics(jobs, engine):
@@ -188,6 +197,7 @@ def tile_sparstriangularupdate_pa_kernel(
                 else:
                     nc.vector.bn_stats(out=odd_stats[:, i, :], in_=values)
 
+            keep_warm(WARM_START)
             for n in range(-2, count + 2):
                 if n + 2 < count:
                     transpose_gate(units[n + 2])
@@ -198,9 +208,11 @@ def tile_sparstriangularupdate_pa_kernel(
                     multiply(units[n])
                 if 0 <= n - 1 < count:
                     quantise(units[n - 1])
-                if 0 <= n - 2:
+                if 0 <= n - 2 and len(banks_after[n - 2]) > 0:
                     for jobs, engine in banks_after[n - 2]:
                         product_statistics(jobs, engine)
+                else:
+                    keep_warm(WARM_ROUND)
 
             junk = junk_pool.tile([P, ROWS], BF16, tag="junk")
             nc.scalar.activation(

@@ -75,16 +75,16 @@ def tile_sparstriangularupdate_pa_kernel(
         codes = {}
         scales = {}
         for side in ("a", "b"):
-            codes[side] = keep.tile([P, CD, ROWS], U32, name="codes_" + side, align_bytes=64)
-            scales[side] = keep.tile([P, CD, ROWS], U8, name="scales_" + side, align_bytes=64)
+            codes[side] = keep.tile([P, BLOCKS, CD, P], U32, name="codes_" + side, align_bytes=64)
+            scales[side] = keep.tile([P, BLOCKS, CD, P], U8, name="scales_" + side, align_bytes=64)
 
-        def product(dst, c, rows, cols, start, stop):
+        def product(dst, r, s, c, start, stop):
             nc.tensor.matmul_mx(
                 out=dst,
-                lhsT=codes["a"][:, c, rows].bitcast(FP8X4),
-                lhsT_scale=scales["a"][:, c, rows],
-                rhs=codes["b"][:, c, cols].bitcast(FP8X4),
-                rhs_scale=scales["b"][:, c, cols],
+                lhsT=codes["a"][:, r, c, :].bitcast(FP8X4),
+                lhsT_scale=scales["a"][:, r, c, :],
+                rhs=codes["b"][:, s, c, :].bitcast(FP8X4),
+                rhs_scale=scales["b"][:, s, c, :],
                 start=start,
                 stop=stop,
             )
@@ -158,13 +158,12 @@ def tile_sparstriangularupdate_pa_kernel(
 
             def quantise(unit):
                 side, r, q = unit
-                rows = slice(r * P, (r + 1) * P)
-                for e in range(2):
-                    nc.vector.quantize_mx(
-                        out=codes[side][:, 2 * q + e, rows].bitcast(FP8X4),
-                        scales=scales[side][:, 2 * q + e, rows],
-                        in_=grouped_of[unit][:, e].rearrange("p i u -> p (i u)"),
-                    )
+                pair = slice(2 * q, 2 * q + 2)
+                nc.vector.quantize_mx(
+                    out=codes[side][:, r, pair, :].rearrange("p e i -> p (e i)").bitcast(FP8X4),
+                    scales=scales[side][:, r, pair, :].rearrange("p e i -> p (e i)"),
+                    in_=grouped_of[unit][:].rearrange("p e i u -> p (e i u)"),
+                )
 
             def keep_warm(times):
                 unread = psum_k.tile([P, BANK_JOBS, P], F32, tag="k")
@@ -180,12 +179,10 @@ def tile_sparstriangularupdate_pa_kernel(
                 done[engine] = i + 1
                 k = psum_k.tile([P, BANK_JOBS, P], F32, tag="k")
                 for x, (r, s, c) in enumerate(jobs):
-                    rows = slice(r * P, (r + 1) * P)
-                    cols = slice(s * P, (s + 1) * P)
-                    product(k[:, x, :], c, rows, cols, True, True)
+                    product(k[:, x, :], r, s, c, True, True)
                     if engine == "scalar":
                         product(
-                            k_sum[:], c, rows, cols, i == 0 and x == 0,
+                            k_sum[:], r, s, c, i == 0 and x == 0,
                             i == scalar_banks - 1 and x == BANK_JOBS - 1,
                         )
                 values = k[:].rearrange("p x j -> p (x j)")
@@ -235,10 +232,7 @@ def tile_sparstriangularupdate_pa_kernel(
             for h in range(2):
                 bank = psum_o.tile([P, HALF, P], F32, tag="bank")
                 for x in range(HALF):
-                    product(
-                        bank[:, x, :], h * HALF + x, slice(r * P, (r + 1) * P),
-                        slice(s * P, (s + 1) * P), True, True,
-                    )
+                    product(bank[:, x, :], r, s, h * HALF + x, True, True)
                 banks_of[n].append(bank)
 
         for n in range(AHEAD):

@@ -27,6 +27,7 @@ COUNT = ROWS * ROWS * CD
 BLOCK_F32 = 8
 WARM_START = 6
 WARM_ROUND = 2
+STORE_BLOCKS = 2
 AHEAD = 2
 
 FLOPS = 2 * ROWS * ROWS * LT * CD
@@ -267,11 +268,13 @@ def tile_sparstriangularupdate_pa_kernel(
 
         for n in range(BLOCKS * BLOCKS):
             r, s = divmod(n, BLOCKS)
-            result = out_pool.tile([P, P, CD], F32, tag="result")
+            part = s % STORE_BLOCKS
+            if part == 0:
+                result = out_pool.tile([P, STORE_BLOCKS * P, CD], F32, tag="result")
             for h in range(2):
                 src = banks_of[n][h][:].rearrange("p x j -> p j x")
-                dst = result[:, :, h * HALF : (h + 1) * HALF]
-                if n % 2 == 0:
+                dst = result[:, part * P : (part + 1) * P, h * HALF : (h + 1) * HALF]
+                if h == 0:
                     nc.vector.tensor_scalar(
                         out=dst, in0=src, scalar1=gain[:, 0:1], scalar2=shift[:, 0:1],
                         op0=ALU.mult, op1=ALU.add,
@@ -280,9 +283,11 @@ def tile_sparstriangularupdate_pa_kernel(
                     nc.scalar.activation(
                         out=dst, in_=src, func=ACT.Identity, bias=shift[:, 0:1], scale=gain[:, 0:1]
                     )
-            nc.sync.dma_start(
-                out=out[0, r * P : (r + 1) * P, s * P : (s + 1) * P, :].rearrange("p j c -> p (j c)"),
-                in_=result[:].rearrange("p j c -> p (j c)"),
-            )
+            if part == STORE_BLOCKS - 1:
+                columns = slice((s - part) * P, (s + 1) * P)
+                nc.sync.dma_start(
+                    out=out[0, r * P : (r + 1) * P, columns, :].rearrange("p j c -> p (j c)"),
+                    in_=result[:].rearrange("p j c -> p (j c)"),
+                )
             if n + AHEAD < BLOCKS * BLOCKS:
                 form_products(n + AHEAD)

@@ -27,7 +27,6 @@ COUNT = ROWS * ROWS * CD
 BLOCK_F32 = 8
 WARM_START = 6
 WARM_ROUND = 2
-STORE_BLOCKS = 2
 AHEAD = 2
 
 FLOPS = 2 * ROWS * ROWS * LT * CD
@@ -266,28 +265,29 @@ def tile_sparstriangularupdate_pa_kernel(
             out=shift[:], in0=neg_mean[:], scalar=gain[:, 0:1], in1=beta_bf[:], op0=ALU.mult, op1=ALU.add
         )
 
-        for n in range(BLOCKS * BLOCKS):
-            r, s = divmod(n, BLOCKS)
-            part = s % STORE_BLOCKS
-            if part == 0:
-                result = out_pool.tile([P, STORE_BLOCKS * P, CD], F32, tag="result")
-            for h in range(2):
-                src = banks_of[n][h][:].rearrange("p x j -> p j x")
-                dst = result[:, part * P : (part + 1) * P, h * HALF : (h + 1) * HALF]
-                if h == 0:
-                    nc.vector.tensor_scalar(
-                        out=dst, in0=src, scalar1=gain[:, 0:1], scalar2=shift[:, 0:1],
-                        op0=ALU.mult, op1=ALU.add,
-                    )
-                else:
-                    nc.scalar.activation(
-                        out=dst, in_=src, func=ACT.Identity, bias=shift[:, 0:1], scale=gain[:, 0:1]
-                    )
-            if part == STORE_BLOCKS - 1:
-                columns = slice((s - part) * P, (s + 1) * P)
-                nc.sync.dma_start(
-                    out=out[0, r * P : (r + 1) * P, columns, :].rearrange("p j c -> p (j c)"),
-                    in_=result[:].rearrange("p j c -> p (j c)"),
-                )
-            if n + AHEAD < BLOCKS * BLOCKS:
-                form_products(n + AHEAD)
+        stores = [(0, [0]), (0, [1]), (0, [2, 3])]
+        for r in range(1, BLOCKS):
+            stores.extend([(r, [0, 1]), (r, [2, 3])])
+        for r, group in stores:
+            result = out_pool.tile([P, len(group) * P, CD], F32, tag="result")
+            for part, s in enumerate(group):
+                n = r * BLOCKS + s
+                for h in range(2):
+                    src = banks_of[n][h][:].rearrange("p x j -> p j x")
+                    dst = result[:, part * P : (part + 1) * P, h * HALF : (h + 1) * HALF]
+                    if h == 0:
+                        nc.vector.tensor_scalar(
+                            out=dst, in0=src, scalar1=gain[:, 0:1], scalar2=shift[:, 0:1],
+                            op0=ALU.mult, op1=ALU.add,
+                        )
+                    else:
+                        nc.scalar.activation(
+                            out=dst, in_=src, func=ACT.Identity, bias=shift[:, 0:1], scale=gain[:, 0:1]
+                        )
+                if n + AHEAD < BLOCKS * BLOCKS:
+                    form_products(n + AHEAD)
+            columns = slice(group[0] * P, (group[-1] + 1) * P)
+            nc.sync.dma_start(
+                out=out[0, r * P : (r + 1) * P, columns, :].rearrange("p j c -> p (j c)"),
+                in_=result[:].rearrange("p j c -> p (j c)"),
+            )

from contextlib import ExitStack

import concourse.mybir as mybir
from concourse.masks import make_identity

F32 = mybir.dt.float32
BF16 = mybir.dt.bfloat16
U32 = mybir.dt.uint32
U8 = mybir.dt.uint8
FP8X4 = mybir.dt.float8_e4m3fn_x4
ACT = mybir.ActivationFunctionType
ALU = mybir.AluOpType
AX = mybir.AxisListType

P = 128
ROWS = 512
LT = 512
CD = 8
EPS = 1e-5
BLOCKS = ROWS // P
PACK = 4
PAIRS = CD // 2
HALF = CD // 2
BN_DIM = 6
BANK_JOBS = 4
COUNT = ROWS * ROWS * CD
BLOCK_F32 = 8
WARM_START = 6
WARM_ROUND = 2
AHEAD = 2

FLOPS = 2 * ROWS * ROWS * LT * CD


def tile_sparstriangularupdate_pa_kernel(
    tc, gate_a, lin_a, gate_b, lin_b, alpha_o, beta_o, out
):
    nc = tc.nc
    with ExitStack() as ctx:
        ctx.enter_context(tc.manual_schedule())
        const = ctx.enter_context(tc.tile_pool(name="const", bufs=1))
        keep = ctx.enter_context(tc.tile_pool(name="keep", bufs=1))

        ident = const.tile([P, P], F32)
        make_identity(nc, ident[:])
        block_order = [(side, r) for r in range(BLOCKS) for side in ("b", "a")]
        units = [(side, r, q) for side, r in block_order for q in range(PAIRS)]
        count = len(units)
        banks_after = []
        waiting = []
        for n, (side, r, q) in enumerate(units):
            partners = [x for other, x in block_order[: n // PAIRS] if other != side]
            for x in partners:
                for e in range(2):
                    waiting.append((r, x, 2 * q + e) if side == "a" else (x, r, 2 * q + e))
            full = []
            while len(waiting) >= BANK_JOBS:
                full.append((waiting[:BANK_JOBS], "scalar" if len(full) == 0 else "vector"))
                waiting = waiting[BANK_JOBS:]
            banks_after.append(full)
        assert len(waiting) == 0
        scalar_banks = sum(1 for full in banks_after for bank in full if bank[1] == "scalar")
        vector_banks = sum(1 for full in banks_after for bank in full if bank[1] == "vector")
        vector_count = vector_banks * BANK_JOBS * P

        even_weights = const.tile([P, P], F32)
        nc.vector.memset(even_weights[:], 1.0 / COUNT)
        odd_weights = const.tile([P, P], F32)
        nc.vector.memset(odd_weights[:], float(vector_count) / COUNT)
        minus_half = const.tile([P, 1], F32)
        nc.vector.memset(minus_half[:], -0.5)
        alpha_bf = const.tile([P, 1], BF16)
        beta_bf = const.tile([P, 1], BF16)

        codes = {}
        scales = {}
        for side in ("a", "b"):
            codes[side] = keep.tile([P, BLOCKS, CD, P], U32, name="codes_" + side, align_bytes=64)
            scales[side] = keep.tile([P, BLOCKS, CD, P], U8, name="scales_" + side, align_bytes=64)

        def product(dst, r, s, c, start, stop):
            nc.tensor.matmul_mx(
                out=dst,
                lhsT=codes["a"][:, r, c, :].bitcast(FP8X4),
                lhsT_scale=scales["a"][:, r, c, :],
                rhs=codes["b"][:, s, c, :].bitcast(FP8X4),
                rhs_scale=scales["b"][:, s, c, :],
                start=start,
                stop=stop,
            )

        odd_stats = keep.tile([P, vector_banks, BN_DIM], F32)
        square_sums = keep.tile([P, scalar_banks], F32)
        odd = keep.tile([P, 2], F32)
        even = keep.tile([P, 2, BLOCK_F32], F32)

        with ExitStack() as first:
            raw = first.enter_context(tc.tile_pool(name="raw", bufs=1))
            sig_pool = first.enter_context(tc.tile_pool(name="sig", bufs=4))
            grp_pool = first.enter_context(tc.tile_pool(name="grp", bufs=3))
            junk_pool = first.enter_context(tc.tile_pool(name="junk", bufs=3))
            psum_t = first.enter_context(tc.psum_pool(name="psum_t", bufs=2))
            psum_k = first.enter_context(tc.psum_pool(name="psum_k", bufs=3))
            psum_s = first.enter_context(tc.psum_pool(name="psum_s", bufs=1))
            k_sum = psum_s.tile([P, P], F32)

            gate_sb = {}
            lin_sb = {}
            for side, r in block_order:
                gate, lin = (gate_b, lin_b) if side == "b" else (gate_a, lin_a)
                rows = slice(r * P, (r + 1) * P)
                g = raw.tile([P, LT * CD], BF16, name="gate_%s%d" % (side, r))
                nc.sync.dma_start(out=g[:], in_=gate[0, rows].rearrange("p t c -> p (t c)"))
                l = raw.tile([P, LT * CD], BF16, name="lin_%s%d" % (side, r))
                nc.sync.dma_start(out=l[:], in_=lin[0, rows].rearrange("p t c -> p (t c)"))
                gate_sb[side, r] = g
                lin_sb[side, r] = l
            with nc.allow_non_contiguous_dma(reason="one scalar to every partition"):
                nc.sync.dma_start(out=alpha_bf[:], in_=alpha_o.partition_broadcast(P))
                nc.sync.dma_start(out=beta_bf[:], in_=beta_o.partition_broadcast(P))

            gate_t_of = {}
            lin_t_of = {}
            sig_of = {}
            grouped_of = {}

            def transpose_words(src, dst, q):
                words = src[:].bitcast(F32).rearrange("p (u t q) -> p u q t", u=PACK, q=PAIRS)
                for u in range(PACK):
                    nc.tensor.transpose(dst[:, u * P : (u + 1) * P], words[:, u, q, :], ident[:])

            def by_channel(bank):
                return bank[:].bitcast(BF16).rearrange("p (u i e) -> p e i u", u=PACK, e=2)

            def transpose_gate(unit):
                side, r, q = unit
                gate_t = psum_t.tile([P, PACK * P], F32, tag="gate_t")
                transpose_words(gate_sb[side, r], gate_t, q)
                gate_t_of[unit] = gate_t

            def transpose_lin(unit):
                side, r, q = unit
                lin_t = psum_t.tile([P, PACK * P], F32, tag="lin_t")
                transpose_words(lin_sb[side, r], lin_t, q)
                lin_t_of[unit] = lin_t

            def sigmoid(unit):
                sig = sig_pool.tile([P, 2, P, PACK], F32, tag="sig")
                nc.scalar.activation(out=sig[:], in_=by_channel(gate_t_of[unit]), func=ACT.Sigmoid)
                sig_of[unit] = sig

            def multiply(unit):
                grouped = grp_pool.tile([P, 2, P, PACK], BF16, tag="grouped", align_bytes=64)
                nc.vector.tensor_tensor(
                    out=grouped[:], in0=sig_of[unit][:], in1=by_channel(lin_t_of[unit]), op=ALU.mult
                )
                grouped_of[unit] = grouped

            def quantise(unit):
                side, r, q = unit
                pair = slice(2 * q, 2 * q + 2)
                nc.vector.quantize_mx(
                    out=codes[side][:, r, pair, :].rearrange("p e i -> p (e i)").bitcast(FP8X4),
                    scales=scales[side][:, r, pair, :].rearrange("p e i -> p (e i)"),
                    in_=grouped_of[unit][:].rearrange("p e i u -> p (e i u)"),
                )

            def keep_warm(times):
                unread = psum_k.tile([P, BANK_JOBS, P], F32, tag="k")
                for x in range(times):
                    nc.tensor.matmul(
                        out=unread[:, x % BANK_JOBS, :], lhsT=ident[:], rhs=ident[:], start=True, stop=True
                    )

            done = {"scalar": 0, "vector": 0}

            def product_statistics(jobs, engine):
                i = done[engine]
                done[engine] = i + 1
                k = psum_k.tile([P, BANK_JOBS, P], F32, tag="k")
                for x, (r, s, c) in enumerate(jobs):
                    product(k[:, x, :], r, s, c, True, True)
                    if engine == "scalar":
                        product(
                            k_sum[:], r, s, c, i == 0 and x == 0,
                            i == scalar_banks - 1 and x == BANK_JOBS - 1,
                        )
                values = k[:].rearrange("p x j -> p (x j)")
                if engine == "scalar":
                    junk = junk_pool.tile([P, ROWS], BF16, tag="junk")
                    nc.scalar.activation(
                        out=junk[:], in_=values, func=ACT.Square, accum_out=square_sums[:, i : i + 1]
                    )
                else:
                    nc.vector.bn_stats(out=odd_stats[:, i, :], in_=values)

            keep_warm(WARM_START)
            for n in range(-2, count + 2):
                if n + 2 < count:
                    transpose_gate(units[n + 2])
                    sigmoid(units[n + 2])
                if 0 <= n + 1 < count:
                    transpose_lin(units[n + 1])
                if 0 <= n < count:
                    multiply(units[n])
                if 0 <= n - 1 < count:
                    quantise(units[n - 1])
                if 0 <= n - 2 and len(banks_after[n - 2]) > 0:
                    for jobs, engine in banks_after[n - 2]:
                        product_statistics(jobs, engine)
                else:
                    keep_warm(WARM_ROUND)

            junk = junk_pool.tile([P, ROWS], BF16, tag="junk")
            nc.scalar.activation(
                out=junk[:, 0:P], in_=k_sum[:], func=ACT.Identity, accum_out=even[:, 0, 0:1]
            )
            nc.vector.bn_aggr(out=odd[:], in_=odd_stats[:].rearrange("p n s -> p (n s)"))
            nc.vector.scalar_tensor_tensor(
                out=odd[:, 1:2], in0=odd[:, 0:1], scalar=odd[:, 0:1], in1=odd[:, 1:2],
                op0=ALU.mult, op1=ALU.add,
            )
            nc.vector.tensor_reduce(out=even[:, 1, 0:1], in_=square_sums[:], axis=AX.X, op=ALU.add)

        psum_o = ctx.enter_context(tc.psum_pool(name="psum_o", bufs=8, reuse_waits="tile"))
        out_pool = ctx.enter_context(tc.tile_pool(name="out_sb", bufs=4, reuse_waits="tile"))
        banks_of = {}

        def form_products(n):
            r, s = divmod(n, BLOCKS)
            banks_of[n] = []
            for h in range(2):
                bank = psum_o.tile([P, HALF, P], F32, tag="bank")
                for x in range(HALF):
                    product(bank[:, x, :], r, s, h * HALF + x, True, True)
                banks_of[n].append(bank)

        for n in range(AHEAD):
            form_products(n)

        total_ps = psum_o.tile([P, 2], F32, tag="bank")
        nc.tensor.matmul(out=total_ps[:], lhsT=odd_weights[:], rhs=odd[:], start=True, stop=False)
        nc.tensor.matmul(
            out=total_ps[:], lhsT=even_weights[:], rhs=even[:, :, 0], start=False, stop=True
        )
        total = keep.tile([P, 2], F32)
        nc.vector.tensor_copy(out=total[:], in_=total_ps[:])
        mean = total[:, 0:1]
        neg_var = keep.tile([P, 1], F32)
        nc.vector.scalar_tensor_tensor(
            out=neg_var[:], in0=mean, scalar=mean, in1=total[:, 1:2], op0=ALU.mult, op1=ALU.subtract
        )
        var_eps = keep.tile([P, 1], F32)
        nc.vector.tensor_scalar(
            out=var_eps[:], in0=neg_var[:], scalar1=-1.0, scalar2=EPS, op0=ALU.mult, op1=ALU.add
        )
        rstd = keep.tile([P, 1], F32)
        nc.gpsimd.tensor_tensor(out=rstd[:], in0=var_eps[:], in1=minus_half[:], op=ALU.pow)
        neg_mean = keep.tile([P, 1], F32)
        nc.vector.tensor_scalar(out=neg_mean[:], in0=mean, scalar1=-1.0, scalar2=None, op0=ALU.mult)
        gain = keep.tile([P, 1], F32)
        nc.vector.tensor_tensor(out=gain[:], in0=rstd[:], in1=alpha_bf[:], op=ALU.mult)
        shift = keep.tile([P, 1], F32)
        nc.vector.scalar_tensor_tensor(
            out=shift[:], in0=neg_mean[:], scalar=gain[:, 0:1], in1=beta_bf[:], op0=ALU.mult, op1=ALU.add
        )

        stores = [(0, [0]), (0, [1]), (0, [2, 3])]
        for r in range(1, BLOCKS):
            stores.extend([(r, [0, 1]), (r, [2, 3])])
        for r, group in stores:
            result = out_pool.tile([P, len(group) * P, CD], F32, tag="result")
            for part, s in enumerate(group):
                n = r * BLOCKS + s
                for h in range(2):
                    src = banks_of[n][h][:].rearrange("p x j -> p j x")
                    dst = result[:, part * P : (part + 1) * P, h * HALF : (h + 1) * HALF]
                    if h == 0:
                        nc.vector.tensor_scalar(
                            out=dst, in0=src, scalar1=gain[:, 0:1], scalar2=shift[:, 0:1],
                            op0=ALU.mult, op1=ALU.add,
                        )
                    else:
                        nc.scalar.activation(
                            out=dst, in_=src, func=ACT.Identity, bias=shift[:, 0:1], scale=gain[:, 0:1]
                        )
                if n + AHEAD < BLOCKS * BLOCKS:
                    form_products(n + AHEAD)
            columns = slice(group[0] * P, (group[-1] + 1) * P)
            nc.sync.dma_start(
                out=out[0, r * P : (r + 1) * P, columns, :].rearrange("p j c -> p (j c)"),
                in_=result[:].rearrange("p j c -> p (j c)"),
            )
